import numpy as np
import ml_dtypes

BF16 = ml_dtypes.bfloat16


def bf(x):
    return np.asarray(x, np.float32).astype(BF16)


def f32(x):
    return np.asarray(x, np.float32)


def f64(x):
    return np.asarray(x).astype(np.float64)


def striped(idx):
    return np.tile(idx.reshape(-1, 16).T, (8, 1))


C, S, NEG, N = 128, 1024, 4, 4096


def setup_inputs():
    return {"z": bf(np.random.standard_normal((C, S))), "w": bf(np.random.standard_normal((C, C)) / np.sqrt(C)), "c": f32(0.1 * np.random.standard_normal((C, S))), "offs": striped(np.concatenate([np.random.permutation(S) for _ in range(N // S)]))}


def reference(z, w, c, offs):
    idx = offs[:16].T.reshape(-1)
    zz, ww, cc = f64(z), f64(w), f64(c)
    pos = (cc * (ww.T @ zz)).sum(axis=0)
    neg = (np.repeat(cc, NEG, axis=1) * (ww.T @ zz[:, idx])).sum(axis=0).reshape(S, NEG)
    return (np.log(np.exp(pos) + np.exp(neg).sum(axis=1)) - pos)[None, :]

@@ -1,0 +1,118 @@
+import concourse.mybir as mybir
+from concourse.masks import make_identity
+
+BF16, F32, U16 = mybir.dt.bfloat16, mybir.dt.float32, mybir.dt.uint16
+MULT, SUBTRACT, ADD, MAX = (
+    mybir.AluOpType.mult,
+    mybir.AluOpType.subtract,
+    mybir.AluOpType.add,
+    mybir.AluOpType.max,
+)
+EXP, LN = mybir.ActivationFunctionType.Exp, mybir.ActivationFunctionType.Ln
+X = mybir.AxisListType.X
+
+CHANNELS = 128
+PATCHES = 1024
+NEGATIVES = 4
+TERMS = NEGATIVES + 1
+ENTRIES = PATCHES * NEGATIVES
+PIECE = 512
+PIECES = ENTRIES // PIECE
+BLOCK = PIECE // NEGATIVES
+HALVES = PATCHES // PIECE
+PSUM_BANKS = 8
+
+FLOPS = 2 * CHANNELS * CHANNELS * (ENTRIES + PATCHES) + 2 * CHANNELS * (ENTRIES + PATCHES)
+
+
+def tile_infonce_loss_kernel(tc, z, w, c, offs, out):
+    nc = tc.nc
+    with (
+        tc.tile_pool(name="held", bufs=1) as held,
+        tc.psum_pool(name="banks", bufs=PSUM_BANKS) as banks,
+    ):
+        offsets = held.tile([CHANNELS, ENTRIES // 16], U16, name="offsets")
+        nc.sync.dma_start(offsets[:], offs)
+        weights = held.tile([CHANNELS, CHANNELS], BF16, name="weights")
+        nc.scalar.dma_start(weights[:], w)
+        store = held.tile([CHANNELS, PATCHES], BF16, name="store")
+        nc.scalar.dma_start(store[:], z)
+        context = held.tile([CHANNELS, PATCHES], F32, name="context")
+        nc.sync.dma_start(context[:, 0:PIECE], c[:, 0:PIECE])
+        nc.gpsimd.dma_start(context[:, PIECE:PATCHES], c[:, PIECE:PATCHES])
+
+        ones = held.tile([CHANNELS, 1], BF16, name="ones")
+        nc.vector.memset(ones[:], 1.0)
+        identity = held.tile([CHANNELS, CHANNELS], F32, name="identity")
+        make_identity(nc, identity[:])
+
+        positive_products = []
+        for half in range(HALVES):
+            columns = slice(half * PIECE, (half + 1) * PIECE)
+            projection = banks.tile([CHANNELS, PIECE], F32, name="projection", tag="bank")
+            nc.tensor.matmul(projection[:], weights[:], store[:, columns], start=True, stop=True)
+            projected = held.tile([CHANNELS, PIECE], F32, name=f"projected{half}")
+            nc.scalar.copy(projected[:], projection[:])
+            product = held.tile([CHANNELS, PIECE], BF16, name=f"positive_product{half}")
+            nc.gpsimd.tensor_tensor(product[:], projected[:], context[:, columns], MULT)
+            positive_products.append(product)
+
+        negative_products = []
+        for b in range(PIECES):
+            picked = store[:].indirect(offsets[:, b * (PIECE // 16) : (b + 1) * (PIECE // 16)])
+            projection = banks.tile([CHANNELS, PIECE], F32, name="projection", tag="bank")
+            nc.tensor.matmul(projection[:], weights[:], picked, start=True, stop=True)
+            product = held.tile([CHANNELS, BLOCK, NEGATIVES], BF16, name=f"negative_product{b}")
+            nc.vector.tensor_tensor(
+                product[:],
+                projection[:].rearrange("o (m n) -> o m n", n=NEGATIVES),
+                context[:, b * BLOCK : (b + 1) * BLOCK]
+                .unsqueeze(2)
+                .to_broadcast([CHANNELS, BLOCK, NEGATIVES]),
+                MULT,
+            )
+            negative_products.append(product)
+
+        scores = banks.tile([BLOCK, PIECES, TERMS], F32, name="scores", tag="bank")
+        for b in range(PIECES):
+            half, q = divmod(b, PIECE // BLOCK)
+            nc.tensor.matmul(
+                scores[:, b, NEGATIVES:TERMS],
+                positive_products[half][:, q * BLOCK : (q + 1) * BLOCK],
+                ones[:],
+                start=True,
+                stop=True,
+            )
+        for b in range(PIECES):
+            for n in range(NEGATIVES):
+                nc.tensor.matmul(
+                    scores[:, b, n : n + 1],
+                    negative_products[b][:, :, n],
+                    ones[:],
+                    start=True,
+                    stop=True,
+                )
+
+        top = held.tile([BLOCK, PIECES], F32, name="top")
+        nc.vector.tensor_reduce(top[:], scores[:], axis=X, op=MAX)
+        shifted = held.tile([BLOCK, PIECES, TERMS], F32, name="shifted")
+        nc.vector.tensor_tensor(
+            shifted[:],
+            scores[:],
+            top[:].unsqueeze(2).to_broadcast([BLOCK, PIECES, TERMS]),
+            SUBTRACT,
+        )
+        powers = held.tile([BLOCK, PIECES, TERMS], F32, name="powers")
+        nc.scalar.activation(powers[:], shifted[:], EXP)
+        total = held.tile([BLOCK, PIECES], F32, name="total")
+        nc.vector.tensor_reduce(total[:], powers[:], axis=X, op=ADD)
+        logsum = held.tile([BLOCK, PIECES], F32, name="logsum")
+        nc.scalar.activation(logsum[:], total[:], LN)
+        loss = held.tile([BLOCK, PIECES], F32, name="loss")
+        nc.vector.tensor_tensor(loss[:], logsum[:], shifted[:, :, NEGATIVES], SUBTRACT)
+
+        flipped = banks.tile([PIECES, BLOCK], F32, name="flipped", tag="bank")
+        nc.tensor.transpose(flipped[:], loss[:], identity[:])
+        rows = held.tile([PIECES, BLOCK], F32, name="rows")
+        nc.vector.tensor_copy(rows[:], flipped[:])
+        nc.sync.dma_start(out.rearrange("one (b m) -> (one b) m", b=PIECES), rows[:])

@@ -21,6 +21,8 @@ PIECES = ENTRIES // PIECE
 BLOCK = PIECE // NEGATIVES
 HALVES = PATCHES // PIECE
 PSUM_BANKS = 8
+STORE_PARTS = 2
+CONTEXT_PARTS = 4
 
 FLOPS = 2 * CHANNELS * CHANNELS * (ENTRIES + PATCHES) + 2 * CHANNELS * (ENTRIES + PATCHES)
 
@@ -35,11 +37,15 @@ def tile_infonce_loss_kernel(tc, z, w, c, offs, out):
         nc.sync.dma_start(offsets[:], offs)
         weights = held.tile([CHANNELS, CHANNELS], BF16, name="weights")
         nc.scalar.dma_start(weights[:], w)
+        queues = (nc.sync, nc.scalar)
         store = held.tile([CHANNELS, PATCHES], BF16, name="store")
-        nc.scalar.dma_start(store[:], z)
+        for part in range(STORE_PARTS):
+            columns = slice(part * PATCHES // STORE_PARTS, (part + 1) * PATCHES // STORE_PARTS)
+            queues[part % 2].dma_start(store[:, columns], z[:, columns])
         context = held.tile([CHANNELS, PATCHES], F32, name="context")
-        nc.sync.dma_start(context[:, 0:PIECE], c[:, 0:PIECE])
-        nc.gpsimd.dma_start(context[:, PIECE:PATCHES], c[:, PIECE:PATCHES])
+        for part in range(CONTEXT_PARTS):
+            columns = slice(part * PATCHES // CONTEXT_PARTS, (part + 1) * PATCHES // CONTEXT_PARTS)
+            queues[part % 2].dma_start(context[:, columns], c[:, columns])
 
         ones = held.tile([CHANNELS, 1], BF16, name="ones")
         nc.vector.memset(ones[:], 1.0)

@@ -112,13 +112,13 @@ def tile_infonce_loss_kernel(tc, z, w, c, offs, out):
         nc.scalar.activation(powers[:], shifted[:], EXP)
         total = held.tile([BLOCK, PIECES], F32, name="total")
         nc.vector.tensor_reduce(total[:], powers[:], axis=X, op=ADD)
-        logsum = held.tile([BLOCK, PIECES], F32, name="logsum")
-        nc.scalar.activation(logsum[:], total[:], LN)
-        loss = held.tile([BLOCK, PIECES], F32, name="loss")
-        nc.vector.tensor_tensor(loss[:], logsum[:], shifted[:, :, NEGATIVES], SUBTRACT)
 
-        flipped = banks.tile([PIECES, BLOCK], F32, name="flipped", tag="bank")
-        nc.tensor.transpose(flipped[:], loss[:], identity[:])
-        rows = held.tile([PIECES, BLOCK], F32, name="rows")
-        nc.vector.tensor_copy(rows[:], flipped[:])
-        nc.sync.dma_start(out.rearrange("one (b m) -> (one b) m", b=PIECES), rows[:])
+        flipped_positive = banks.tile([PIECES, BLOCK], F32, name="flipped_positive", tag="bank")
+        nc.tensor.transpose(flipped_positive[:], shifted[:, :, NEGATIVES], identity[:])
+        flipped_total = banks.tile([PIECES, BLOCK], F32, name="flipped_total", tag="bank")
+        nc.tensor.transpose(flipped_total[:], total[:], identity[:])
+        logsum = held.tile([PIECES, BLOCK], F32, name="logsum")
+        nc.scalar.activation(logsum[:], flipped_total[:], LN)
+        loss = held.tile([PIECES, BLOCK], F32, name="loss")
+        nc.vector.tensor_tensor(loss[:], logsum[:], flipped_positive[:], SUBTRACT)
+        nc.sync.dma_start(out.rearrange("one (b m) -> (one b) m", b=PIECES), loss[:])

@@ -21,6 +21,7 @@ PIECES = ENTRIES // PIECE
 BLOCK = PIECE // NEGATIVES
 HALVES = PATCHES // PIECE
 PSUM_BANKS = 8
+WARM_UP = 4
 STORE_PARTS = 2
 CONTEXT_PARTS = 4
 
@@ -33,19 +34,25 @@ def tile_infonce_loss_kernel(tc, z, w, c, offs, out):
         tc.tile_pool(name="held", bufs=1) as held,
         tc.psum_pool(name="banks", bufs=PSUM_BANKS) as banks,
     ):
-        offsets = held.tile([CHANNELS, ENTRIES // 16], U16, name="offsets")
-        nc.sync.dma_start(offsets[:], offs)
+        queues = (nc.sync, nc.scalar)
         weights = held.tile([CHANNELS, CHANNELS], BF16, name="weights")
         nc.scalar.dma_start(weights[:], w)
-        queues = (nc.sync, nc.scalar)
         store = held.tile([CHANNELS, PATCHES], BF16, name="store")
         for part in range(STORE_PARTS):
             columns = slice(part * PATCHES // STORE_PARTS, (part + 1) * PATCHES // STORE_PARTS)
             queues[part % 2].dma_start(store[:, columns], z[:, columns])
+        offsets = held.tile([CHANNELS, ENTRIES // 16], U16, name="offsets")
+        nc.sync.dma_start(offsets[:], offs)
         context = held.tile([CHANNELS, PATCHES], F32, name="context")
         for part in range(CONTEXT_PARTS):
             columns = slice(part * PATCHES // CONTEXT_PARTS, (part + 1) * PATCHES // CONTEXT_PARTS)
             queues[part % 2].dma_start(context[:, columns], c[:, columns])
+
+        zeros = held.tile([CHANNELS, PIECE], BF16, name="zeros")
+        nc.gpsimd.memset(zeros[:], 0.0)
+        unread = banks.tile([CHANNELS, PIECE], F32, name="unread", tag="bank")
+        for turn in range(WARM_UP):
+            nc.tensor.matmul(unread[:], zeros[:, 0:CHANNELS], zeros[:], start=True, stop=True)
 
         ones = held.tile([CHANNELS, 1], BF16, name="ones")
         nc.vector.memset(ones[:], 1.0)

@@ -21,7 +21,6 @@ PIECES = ENTRIES // PIECE
 BLOCK = PIECE // NEGATIVES
 HALVES = PATCHES // PIECE
 PSUM_BANKS = 8
-WARM_UP = 4
 STORE_PARTS = 2
 CONTEXT_PARTS = 4
 
@@ -34,25 +33,19 @@ def tile_infonce_loss_kernel(tc, z, w, c, offs, out):
         tc.tile_pool(name="held", bufs=1) as held,
         tc.psum_pool(name="banks", bufs=PSUM_BANKS) as banks,
     ):
-        queues = (nc.sync, nc.scalar)
+        offsets = held.tile([CHANNELS, ENTRIES // 16], U16, name="offsets")
+        nc.sync.dma_start(offsets[:], offs)
         weights = held.tile([CHANNELS, CHANNELS], BF16, name="weights")
         nc.scalar.dma_start(weights[:], w)
+        queues = (nc.sync, nc.scalar)
         store = held.tile([CHANNELS, PATCHES], BF16, name="store")
         for part in range(STORE_PARTS):
             columns = slice(part * PATCHES // STORE_PARTS, (part + 1) * PATCHES // STORE_PARTS)
             queues[part % 2].dma_start(store[:, columns], z[:, columns])
-        offsets = held.tile([CHANNELS, ENTRIES // 16], U16, name="offsets")
-        nc.sync.dma_start(offsets[:], offs)
         context = held.tile([CHANNELS, PATCHES], F32, name="context")
         for part in range(CONTEXT_PARTS):
             columns = slice(part * PATCHES // CONTEXT_PARTS, (part + 1) * PATCHES // CONTEXT_PARTS)
             queues[part % 2].dma_start(context[:, columns], c[:, columns])
-
-        zeros = held.tile([CHANNELS, PIECE], BF16, name="zeros")
-        nc.gpsimd.memset(zeros[:], 0.0)
-        unread = banks.tile([CHANNELS, PIECE], F32, name="unread", tag="bank")
-        for turn in range(WARM_UP):
-            nc.tensor.matmul(unread[:], zeros[:, 0:CHANNELS], zeros[:], start=True, stop=True)
 
         ones = held.tile([CHANNELS, 1], BF16, name="ones")
         nc.vector.memset(ones[:], 1.0)
@@ -75,9 +68,9 @@ def tile_infonce_loss_kernel(tc, z, w, c, offs, out):
             picked = store[:].indirect(offsets[:, b * (PIECE // 16) : (b + 1) * (PIECE // 16)])
             projection = banks.tile([CHANNELS, PIECE], F32, name="projection", tag="bank")
             nc.tensor.matmul(projection[:], weights[:], picked, start=True, stop=True)
-            product = held.tile([CHANNELS, BLOCK, NEGATIVES], BF16, name=f"negative_product{b}")
+            product = held.tile([CHANNELS, NEGATIVES, BLOCK], BF16, name=f"negative_product{b}")
             nc.vector.tensor_tensor(
-                product[:],
+                product[:].rearrange("o n m -> o m n"),
                 projection[:].rearrange("o (m n) -> o m n", n=NEGATIVES),
                 context[:, b * BLOCK : (b + 1) * BLOCK]
                 .unsqueeze(2)
@@ -100,7 +93,7 @@ def tile_infonce_loss_kernel(tc, z, w, c, offs, out):
             for n in range(NEGATIVES):
                 nc.tensor.matmul(
                     scores[:, b, n : n + 1],
-                    negative_products[b][:, :, n],
+                    negative_products[b][:, n, :],
                     ones[:],
                     start=True,
                     stop=True,

@@ -52,25 +52,14 @@ def tile_infonce_loss_kernel(tc, z, w, c, offs, out):
         identity = held.tile([CHANNELS, CHANNELS], F32, name="identity")
         make_identity(nc, identity[:])
 
-        positive_products = []
-        for half in range(HALVES):
-            columns = slice(half * PIECE, (half + 1) * PIECE)
-            projection = banks.tile([CHANNELS, PIECE], F32, name="projection", tag="bank")
-            nc.tensor.matmul(projection[:], weights[:], store[:, columns], start=True, stop=True)
-            projected = held.tile([CHANNELS, PIECE], F32, name=f"projected{half}")
-            nc.scalar.copy(projected[:], projection[:])
-            product = held.tile([CHANNELS, PIECE], BF16, name=f"positive_product{half}")
-            nc.gpsimd.tensor_tensor(product[:], projected[:], context[:, columns], MULT)
-            positive_products.append(product)
-
         negative_products = []
         for b in range(PIECES):
             picked = store[:].indirect(offsets[:, b * (PIECE // 16) : (b + 1) * (PIECE // 16)])
             projection = banks.tile([CHANNELS, PIECE], F32, name="projection", tag="bank")
             nc.tensor.matmul(projection[:], weights[:], picked, start=True, stop=True)
-            product = held.tile([CHANNELS, NEGATIVES, BLOCK], BF16, name=f"negative_product{b}")
+            product = held.tile([CHANNELS, BLOCK, NEGATIVES], BF16, name=f"negative_product{b}")
             nc.vector.tensor_tensor(
-                product[:].rearrange("o n m -> o m n"),
+                product[:],
                 projection[:].rearrange("o (m n) -> o m n", n=NEGATIVES),
                 context[:, b * BLOCK : (b + 1) * BLOCK]
                 .unsqueeze(2)
@@ -79,7 +68,25 @@ def tile_infonce_loss_kernel(tc, z, w, c, offs, out):
             )
             negative_products.append(product)
 
+        positive_products = []
+        for half in range(HALVES):
+            columns = slice(half * PIECE, (half + 1) * PIECE)
+            projection = banks.tile([CHANNELS, PIECE], F32, name="projection", tag="bank")
+            nc.tensor.matmul(projection[:], weights[:], store[:, columns], start=True, stop=True)
+            product = held.tile([CHANNELS, PIECE], BF16, name=f"positive_product{half}")
+            nc.vector.tensor_tensor(product[:], projection[:], context[:, columns], MULT)
+            positive_products.append(product)
+
         scores = banks.tile([BLOCK, PIECES, TERMS], F32, name="scores", tag="bank")
+        for b in range(PIECES):
+            for n in range(NEGATIVES):
+                nc.tensor.matmul(
+                    scores[:, b, n : n + 1],
+                    negative_products[b][:, :, n],
+                    ones[:],
+                    start=True,
+                    stop=True,
+                )
         for b in range(PIECES):
             half, q = divmod(b, PIECE // BLOCK)
             nc.tensor.matmul(
@@ -89,15 +96,6 @@ def tile_infonce_loss_kernel(tc, z, w, c, offs, out):
                 start=True,
                 stop=True,
             )
-        for b in range(PIECES):
-            for n in range(NEGATIVES):
-                nc.tensor.matmul(
-                    scores[:, b, n : n + 1],
-                    negative_products[b][:, n, :],
-                    ones[:],
-                    start=True,
-                    stop=True,
-                )
 
         top = held.tile([BLOCK, PIECES], F32, name="top")
         nc.vector.tensor_reduce(top[:], scores[:], axis=X, op=MAX)

@@ -33,15 +33,15 @@ def tile_infonce_loss_kernel(tc, z, w, c, offs, out):
         tc.tile_pool(name="held", bufs=1) as held,
         tc.psum_pool(name="banks", bufs=PSUM_BANKS) as banks,
     ):
-        offsets = held.tile([CHANNELS, ENTRIES // 16], U16, name="offsets")
-        nc.sync.dma_start(offsets[:], offs)
+        queues = (nc.sync, nc.scalar)
         weights = held.tile([CHANNELS, CHANNELS], BF16, name="weights")
         nc.scalar.dma_start(weights[:], w)
-        queues = (nc.sync, nc.scalar)
         store = held.tile([CHANNELS, PATCHES], BF16, name="store")
         for part in range(STORE_PARTS):
             columns = slice(part * PATCHES // STORE_PARTS, (part + 1) * PATCHES // STORE_PARTS)
             queues[part % 2].dma_start(store[:, columns], z[:, columns])
+        offsets = held.tile([CHANNELS, ENTRIES // 16], U16, name="offsets")
+        nc.sync.dma_start(offsets[:], offs)
         context = held.tile([CHANNELS, PATCHES], F32, name="context")
         for part in range(CONTEXT_PARTS):
             columns = slice(part * PATCHES // CONTEXT_PARTS, (part + 1) * PATCHES // CONTEXT_PARTS)
@@ -51,6 +51,17 @@ def tile_infonce_loss_kernel(tc, z, w, c, offs, out):
         nc.vector.memset(ones[:], 1.0)
         identity = held.tile([CHANNELS, CHANNELS], F32, name="identity")
         make_identity(nc, identity[:])
+
+        positive_products = []
+        for half in range(HALVES):
+            columns = slice(half * PIECE, (half + 1) * PIECE)
+            projection = banks.tile([CHANNELS, PIECE], F32, name="projection", tag="bank")
+            nc.tensor.matmul(projection[:], weights[:], store[:, columns], start=True, stop=True)
+            projected = held.tile([CHANNELS, PIECE], F32, name=f"projected{half}")
+            nc.scalar.copy(projected[:], projection[:])
+            product = held.tile([CHANNELS, PIECE], BF16, name=f"positive_product{half}")
+            nc.gpsimd.tensor_tensor(product[:], projected[:], context[:, columns], MULT)
+            positive_products.append(product)
 
         negative_products = []
         for b in range(PIECES):
@@ -68,25 +79,7 @@ def tile_infonce_loss_kernel(tc, z, w, c, offs, out):
             )
             negative_products.append(product)
 
-        positive_products = []
-        for half in range(HALVES):
-            columns = slice(half * PIECE, (half + 1) * PIECE)
-            projection = banks.tile([CHANNELS, PIECE], F32, name="projection", tag="bank")
-            nc.tensor.matmul(projection[:], weights[:], store[:, columns], start=True, stop=True)
-            product = held.tile([CHANNELS, PIECE], BF16, name=f"positive_product{half}")
-            nc.vector.tensor_tensor(product[:], projection[:], context[:, columns], MULT)
-            positive_products.append(product)
-
         scores = banks.tile([BLOCK, PIECES, TERMS], F32, name="scores", tag="bank")
-        for b in range(PIECES):
-            for n in range(NEGATIVES):
-                nc.tensor.matmul(
-                    scores[:, b, n : n + 1],
-                    negative_products[b][:, :, n],
-                    ones[:],
-                    start=True,
-                    stop=True,
-                )
         for b in range(PIECES):
             half, q = divmod(b, PIECE // BLOCK)
             nc.tensor.matmul(
@@ -96,6 +89,15 @@ def tile_infonce_loss_kernel(tc, z, w, c, offs, out):
                 start=True,
                 stop=True,
             )
+        for b in range(PIECES):
+            for n in range(NEGATIVES):
+                nc.tensor.matmul(
+                    scores[:, b, n : n + 1],
+                    negative_products[b][:, :, n],
+                    ones[:],
+                    start=True,
+                    stop=True,
+                )
 
         top = held.tile([BLOCK, PIECES], F32, name="top")
         nc.vector.tensor_reduce(top[:], scores[:], axis=X, op=MAX)

@@ -21,6 +21,7 @@ PIECES = ENTRIES // PIECE
 BLOCK = PIECE // NEGATIVES
 HALVES = PATCHES // PIECE
 PSUM_BANKS = 8
+GPSIMD_PIECE = 3
 STORE_PARTS = 2
 CONTEXT_PARTS = 4
 
@@ -33,15 +34,15 @@ def tile_infonce_loss_kernel(tc, z, w, c, offs, out):
         tc.tile_pool(name="held", bufs=1) as held,
         tc.psum_pool(name="banks", bufs=PSUM_BANKS) as banks,
     ):
-        queues = (nc.sync, nc.scalar)
+        offsets = held.tile([CHANNELS, ENTRIES // 16], U16, name="offsets")
+        nc.sync.dma_start(offsets[:], offs)
         weights = held.tile([CHANNELS, CHANNELS], BF16, name="weights")
         nc.scalar.dma_start(weights[:], w)
+        queues = (nc.sync, nc.scalar)
         store = held.tile([CHANNELS, PATCHES], BF16, name="store")
         for part in range(STORE_PARTS):
             columns = slice(part * PATCHES // STORE_PARTS, (part + 1) * PATCHES // STORE_PARTS)
             queues[part % 2].dma_start(store[:, columns], z[:, columns])
-        offsets = held.tile([CHANNELS, ENTRIES // 16], U16, name="offsets")
-        nc.sync.dma_start(offsets[:], offs)
         context = held.tile([CHANNELS, PATCHES], F32, name="context")
         for part in range(CONTEXT_PARTS):
             columns = slice(part * PATCHES // CONTEXT_PARTS, (part + 1) * PATCHES // CONTEXT_PARTS)
@@ -68,10 +69,16 @@ def tile_infonce_loss_kernel(tc, z, w, c, offs, out):
             picked = store[:].indirect(offsets[:, b * (PIECE // 16) : (b + 1) * (PIECE // 16)])
             projection = banks.tile([CHANNELS, PIECE], F32, name="projection", tag="bank")
             nc.tensor.matmul(projection[:], weights[:], picked, start=True, stop=True)
+            if b == GPSIMD_PIECE:
+                projected = held.tile([CHANNELS, PIECE], F32, name=f"projected_piece{b}")
+                nc.scalar.copy(projected[:], projection[:])
+                multiplier, factor = nc.gpsimd, projected
+            else:
+                multiplier, factor = nc.vector, projection
             product = held.tile([CHANNELS, BLOCK, NEGATIVES], BF16, name=f"negative_product{b}")
-            nc.vector.tensor_tensor(
+            multiplier.tensor_tensor(
                 product[:],
-                projection[:].rearrange("o (m n) -> o m n", n=NEGATIVES),
+                factor[:].rearrange("o (m n) -> o m n", n=NEGATIVES),
                 context[:, b * BLOCK : (b + 1) * BLOCK]
                 .unsqueeze(2)
                 .to_broadcast([CHANNELS, BLOCK, NEGATIVES]),

import concourse.mybir as mybir
from concourse.masks import make_identity

BF16, F32, U16 = mybir.dt.bfloat16, mybir.dt.float32, mybir.dt.uint16
MULT, SUBTRACT, ADD, MAX = (
    mybir.AluOpType.mult,
    mybir.AluOpType.subtract,
    mybir.AluOpType.add,
    mybir.AluOpType.max,
)
EXP, LN = mybir.ActivationFunctionType.Exp, mybir.ActivationFunctionType.Ln
X = mybir.AxisListType.X

CHANNELS = 128
PATCHES = 1024
NEGATIVES = 4
TERMS = NEGATIVES + 1
ENTRIES = PATCHES * NEGATIVES
PIECE = 512
PIECES = ENTRIES // PIECE
BLOCK = PIECE // NEGATIVES
HALVES = PATCHES // PIECE
PSUM_BANKS = 8
GPSIMD_PIECE = 3
STORE_PARTS = 2
CONTEXT_PARTS = 4

FLOPS = 2 * CHANNELS * CHANNELS * (ENTRIES + PATCHES) + 2 * CHANNELS * (ENTRIES + PATCHES)


def tile_infonce_loss_kernel(tc, z, w, c, offs, out):
    nc = tc.nc
    with (
        tc.tile_pool(name="held", bufs=1) as held,
        tc.psum_pool(name="banks", bufs=PSUM_BANKS) as banks,
    ):
        offsets = held.tile([CHANNELS, ENTRIES // 16], U16, name="offsets")
        nc.sync.dma_start(offsets[:], offs)
        weights = held.tile([CHANNELS, CHANNELS], BF16, name="weights")
        nc.scalar.dma_start(weights[:], w)
        queues = (nc.sync, nc.scalar)
        store = held.tile([CHANNELS, PATCHES], BF16, name="store")
        for part in range(STORE_PARTS):
            columns = slice(part * PATCHES // STORE_PARTS, (part + 1) * PATCHES // STORE_PARTS)
            queues[part % 2].dma_start(store[:, columns], z[:, columns])
        context = held.tile([CHANNELS, PATCHES], F32, name="context")
        for part in range(CONTEXT_PARTS):
            columns = slice(part * PATCHES // CONTEXT_PARTS, (part + 1) * PATCHES // CONTEXT_PARTS)
            queues[part % 2].dma_start(context[:, columns], c[:, columns])

        ones = held.tile([CHANNELS, 1], BF16, name="ones")
        nc.vector.memset(ones[:], 1.0)
        identity = held.tile([CHANNELS, CHANNELS], F32, name="identity")
        make_identity(nc, identity[:])

        positive_products = []
        for half in range(HALVES):
            columns = slice(half * PIECE, (half + 1) * PIECE)
            projection = banks.tile([CHANNELS, PIECE], F32, name="projection", tag="bank")
            nc.tensor.matmul(projection[:], weights[:], store[:, columns], start=True, stop=True)
            projected = held.tile([CHANNELS, PIECE], F32, name=f"projected{half}")
            nc.scalar.copy(projected[:], projection[:])
            product = held.tile([CHANNELS, PIECE], BF16, name=f"positive_product{half}")
            nc.gpsimd.tensor_tensor(product[:], projected[:], context[:, columns], MULT)
            positive_products.append(product)

        negative_products = []
        for b in range(PIECES):
            picked = store[:].indirect(offsets[:, b * (PIECE // 16) : (b + 1) * (PIECE // 16)])
            projection = banks.tile([CHANNELS, PIECE], F32, name="projection", tag="bank")
            nc.tensor.matmul(projection[:], weights[:], picked, start=True, stop=True)
            if b == GPSIMD_PIECE:
                projected = held.tile([CHANNELS, PIECE], F32, name=f"projected_piece{b}")
                nc.scalar.copy(projected[:], projection[:])
                multiplier, factor = nc.gpsimd, projected
            else:
                multiplier, factor = nc.vector, projection
            product = held.tile([CHANNELS, BLOCK, NEGATIVES], BF16, name=f"negative_product{b}")
            multiplier.tensor_tensor(
                product[:],
                factor[:].rearrange("o (m n) -> o m n", n=NEGATIVES),
                context[:, b * BLOCK : (b + 1) * BLOCK]
                .unsqueeze(2)
                .to_broadcast([CHANNELS, BLOCK, NEGATIVES]),
                MULT,
            )
            negative_products.append(product)

        scores = banks.tile([BLOCK, PIECES, TERMS], F32, name="scores", tag="bank")
        for b in range(PIECES):
            half, q = divmod(b, PIECE // BLOCK)
            nc.tensor.matmul(
                scores[:, b, NEGATIVES:TERMS],
                positive_products[half][:, q * BLOCK : (q + 1) * BLOCK],
                ones[:],
                start=True,
                stop=True,
            )
        for b in range(PIECES):
            for n in range(NEGATIVES):
                nc.tensor.matmul(
                    scores[:, b, n : n + 1],
                    negative_products[b][:, :, n],
                    ones[:],
                    start=True,
                    stop=True,
                )

        top = held.tile([BLOCK, PIECES], F32, name="top")
        nc.vector.tensor_reduce(top[:], scores[:], axis=X, op=MAX)
        shifted = held.tile([BLOCK, PIECES, TERMS], F32, name="shifted")
        nc.vector.tensor_tensor(
            shifted[:],
            scores[:],
            top[:].unsqueeze(2).to_broadcast([BLOCK, PIECES, TERMS]),
            SUBTRACT,
        )
        powers = held.tile([BLOCK, PIECES, TERMS], F32, name="powers")
        nc.scalar.activation(powers[:], shifted[:], EXP)
        total = held.tile([BLOCK, PIECES], F32, name="total")
        nc.vector.tensor_reduce(total[:], powers[:], axis=X, op=ADD)

        flipped_positive = banks.tile([PIECES, BLOCK], F32, name="flipped_positive", tag="bank")
        nc.tensor.transpose(flipped_positive[:], shifted[:, :, NEGATIVES], identity[:])
        flipped_total = banks.tile([PIECES, BLOCK], F32, name="flipped_total", tag="bank")
        nc.tensor.transpose(flipped_total[:], total[:], identity[:])
        logsum = held.tile([PIECES, BLOCK], F32, name="logsum")
        nc.scalar.activation(logsum[:], flipped_total[:], LN)
        loss = held.tile([PIECES, BLOCK], F32, name="loss")
        nc.vector.tensor_tensor(loss[:], logsum[:], flipped_positive[:], SUBTRACT)
        nc.sync.dma_start(out.rearrange("one (b m) -> (one b) m", b=PIECES), loss[:])
